import numpy as np
import ml_dtypes


def mxq(x, axis, fmt="e4m3"):
    dtype, down = {"e4m3": (ml_dtypes.float8_e4m3fn, 7), "e5m2": (ml_dtypes.float8_e5m2, 14)}[fmt]
    v = np.moveaxis(np.asarray(x, np.float32).astype(ml_dtypes.bfloat16).astype(np.float64), axis, -1)
    blocks = v.reshape(v.shape[:-1] + (-1, 32))
    amax = np.abs(blocks).max(-1, keepdims=True)
    byte = np.maximum(np.where(amax > 0, np.frexp(amax)[1] - 1 + 127, 0) - down, 1)
    scale = np.exp2(byte - 127.0)
    codes = (blocks / scale).astype(np.float32).astype(dtype).astype(np.float64)
    return np.moveaxis((codes * scale).reshape(v.shape), -1, axis)


WIDE = False


def mx_kscale(k):
    if not WIDE:
        return np.ones(k)
    levels = np.array([10, -10, 5, -5, 0])
    a = np.random.permutation(np.resize(levels, k // 512 * 4)).reshape(k // 512, 4)
    idx = np.arange(k)
    return np.exp2(a[idx // 512, idx % 128 // 32])


BF16 = ml_dtypes.bfloat16


def bf(x):
    return np.asarray(x, np.float32).astype(BF16)


def f64(x):
    return np.asarray(x).astype(np.float64)


E2M1 = np.array([0.0, 0.5, 1.0, 1.5, 2.0, 3.0, 4.0, 6.0, -0.0, -0.5, -1.0, -1.5, -2.0, -3.0, -4.0, -6.0])


def pack_weight(w, fmt):
    k, n = w.shape
    w = f64(bf(w)).reshape(k // 32, 32, n)
    amax = np.abs(w).max(1)
    if fmt == "e4m3":
        byte = np.frexp(amax)[1] - 1 + 127 - 7
    else:
        mant, ex = np.frexp(amax / 6.0)
        byte = np.where(mant > 0.5, ex, ex - 1) + 127
    byte = np.clip(np.where(amax > 0, byte, 1), 1, 254)
    scaled = (w * np.exp2(127.0 - byte)[:, None, :]).reshape(k, n).astype(np.float32)
    by_word = np.ascontiguousarray(scaled.reshape(k // 512, 128, 4, n).transpose(0, 1, 3, 2))
    if fmt == "e4m3":
        words = by_word.astype(ml_dtypes.float8_e4m3fn).view(np.uint8)
    else:
        c = by_word.astype(ml_dtypes.float4_e2m1fn).view(np.uint8) & 0xF
        words = c[..., 0::2] | (c[..., 1::2] << 4)
    return np.ascontiguousarray(words), np.ascontiguousarray(byte.astype(np.uint8).reshape(k // 512, 16, n))


def unpack_weight(words, scales, fmt):
    g, p, n, _ = words.shape
    if fmt == "e4m3":
        vals = np.ascontiguousarray(words).view(ml_dtypes.float8_e4m3fn).astype(np.float64)
    else:
        nib = np.empty((g, p, n, 4), np.uint8)
        nib[..., 0::2] = words & 0xF
        nib[..., 1::2] = words >> 4
        vals = E2M1[nib]
    vals = vals * np.repeat(np.exp2(scales.astype(np.float64) - 127.0), 8, axis=1)[..., None]
    return vals.transpose(0, 1, 3, 2).reshape(g * 512, n)

def pack4(w):
    words, scales = pack_weight(w, "e2m1")
    return words.reshape(words.shape[0], 128, -1), scales


def unpack4(words, scales):
    return unpack_weight(words.reshape(words.shape[0], 128, -1, 2), scales, "e2m1")


B, IDIM, HDIM, ODIM, S, DEPTH, NACT, NTOP = 1024, 512, 1024, 512, 128, 32, 3, 2


def sigmoid(v):
    return 1.0 / (1.0 + np.exp(-v))


def setup_inputs():
    s, t = mx_kscale(IDIM), mx_kscale(HDIM)
    x = bf(np.random.standard_normal((B, IDIM)) * s)
    hidden = bf(np.random.standard_normal((B, HDIM)) * t)
    stack_top = bf(np.random.standard_normal((B, NTOP, S)))
    Wi = np.random.standard_normal((HDIM, IDIM)) * 0.7 / np.sqrt(IDIM) / s
    bi = bf(np.random.standard_normal(HDIM) * 0.2)
    Wh = np.random.standard_normal((HDIM, HDIM)) * 0.7 / np.sqrt(HDIM) / t
    bh = bf(np.random.standard_normal(HDIM) * 0.2)
    W0 = bf(np.random.standard_normal((HDIM, S)) * 0.5 / np.sqrt(S))
    b0 = bf(np.random.standard_normal(HDIM) * 0.2)
    W1 = bf(np.random.standard_normal((HDIM, S)) * 0.5 / np.sqrt(S))
    b1 = bf(np.random.standard_normal(HDIM) * 0.2)
    Wi_words, Wi_scales = pack4(np.ascontiguousarray(Wi.T))
    Wh_words, Wh_scales = pack4(np.ascontiguousarray(Wh.T))
    return {"x": x,
            "hidden": hidden,
            "stack_top": stack_top,
            "Wi_words": Wi_words,
            "Wi_scales": Wi_scales,
            "bi": bi,
            "Wh_words": Wh_words,
            "Wh_scales": Wh_scales,
            "bh": bh,
            "W0": W0,
            "b0": b0,
            "W1": W1,
            "b1": b1}


def reference(x, hidden, stack_top, Wi_words, Wi_scales, bi, Wh_words, Wh_scales, bh, W0, b0, W1, b1):
    pre = ((mxq(f64(x), 1, "e4m3") @ unpack4(Wi_words, Wi_scales)) + f64(bi)
           + (mxq(f64(hidden), 1, "e4m3") @ unpack4(Wh_words, Wh_scales)) + f64(bh)
           + f64(stack_top)[:, 0] @ f64(W0).T + f64(b0)
           + f64(stack_top)[:, 1] @ f64(W1).T + f64(b1))
    return sigmoid(pre)

@@ -1,0 +1,191 @@
+from contextlib import ExitStack
+
+import concourse.mybir as mybir
+from concourse.masks import make_identity
+
+F32 = mybir.dt.float32
+BF16 = mybir.dt.bfloat16
+I32 = mybir.dt.int32
+U32 = mybir.dt.uint32
+U8 = mybir.dt.uint8
+FP8X4 = mybir.dt.float8_e4m3fn_x4
+FP4X4 = mybir.dt.float4_e2m1fn_x4
+
+P = 128
+BATCH, IDIM, HDIM, S, NTOP = 1024, 512, 1024, 128, 2
+M_TILES = BATCH // P
+N_TILE = 512
+N_TILES = HDIM // N_TILE
+K_PASS = 4 * P
+PASSES = (IDIM + HDIM) // K_PASS
+H_PASSES = HDIM // K_PASS
+PASS_WORDS = K_PASS // 2
+H_BLOCKS = HDIM // P
+
+assert N_TILES == H_PASSES and NTOP == 2
+
+FLOPS = 2 * BATCH * HDIM * (IDIM + HDIM + NTOP * S)
+
+
+def tile_stackrnn_pa_kernel(
+    tc, x, hidden, stack_top, Wi_words, Wi_scales, bi, Wh_words, Wh_scales, bh, W0, b0, W1, b1, out
+):
+    nc = tc.nc
+    add = mybir.AluOpType.add
+    sigmoid = mybir.ActivationFunctionType.Sigmoid
+
+    with ExitStack() as ctx:
+        ctx.enter_context(tc.manual_schedule())
+        keep = ctx.enter_context(tc.tile_pool(name="keep", bufs=1))
+        stage = ctx.enter_context(tc.tile_pool(name="stage", bufs=3))
+        psum_t = ctx.enter_context(tc.psum_pool(name="psum_t", bufs=3))
+        psum_acc = ctx.enter_context(tc.psum_pool(name="psum_acc", bufs=5))
+
+        ident_f32 = keep.tile([P, P], F32)
+        make_identity(nc, ident_f32[:])
+        ident_bf16 = keep.tile([P, P], BF16)
+        make_identity(nc, ident_bf16[:])
+        bias_rows = keep.tile([P, HDIM], BF16)
+        nc.vector.memset(bias_rows[:], 0.0)
+        warm = keep.tile([P, 1], F32)
+        nc.vector.memset(warm[:], 0.0)
+        ones = keep.tile([P, P], BF16)
+        nc.vector.memset(ones[:], 1.0)
+        w_planes = keep.tile([P, PASSES, HDIM], U8, align_bytes=64)
+        nc.vector.memset(w_planes[:].bitcast(I32), 0)
+
+        for row, bias in enumerate((bi, bh, b0, b1)):
+            nc.scalar.dma_start(out=bias_rows[row : row + 1, :], in_=bias.rearrange("(o n) -> o n", o=1))
+        nc.scalar.activation(out=warm[:], in_=warm[:], func=sigmoid)
+
+        x_sb = keep.tile([P, M_TILES, IDIM], BF16)
+        x_rows = x.rearrange("(p m) k -> p m k", m=M_TILES)
+        for pair in range(M_TILES // 2):
+            two = slice(2 * pair, 2 * pair + 2)
+            nc.sync.dma_start(out=x_sb[:, two, :], in_=x_rows[:, two, :])
+
+        st_sb = keep.tile([P, M_TILES, NTOP, S], BF16)
+        nc.sync.dma_start(out=st_sb[:], in_=stack_top.rearrange("(p m) t s -> p m t s", m=M_TILES))
+
+        w_sb = keep.tile([P, NTOP, H_BLOCKS, S], BF16)
+        nc.sync.dma_start(out=w_sb[:, 0, :, :], in_=W0.rearrange("(j p) s -> p j s", p=P))
+        nc.sync.dma_start(out=w_sb[:, 1, :, :], in_=W1.rearrange("(j p) s -> p j s", p=P))
+
+        h_sb = keep.tile([P, M_TILES, HDIM], BF16)
+        h_rows = hidden.rearrange("(p m) k -> p m k", m=M_TILES)
+        for pair in range(M_TILES // 2):
+            two = slice(2 * pair, 2 * pair + 2)
+            nc.sync.dma_start(out=h_sb[:, two, :], in_=h_rows[:, two, :])
+
+        w_words = keep.tile([P, PASSES, 2 * HDIM], U8, align_bytes=64)
+        nc.sync.dma_start(out=w_words[:, 0, :].bitcast(I32), in_=Wi_words.bitcast(I32)[0])
+        nc.sync.dma_start(
+            out=w_words[:, 1:PASSES, :].bitcast(I32), in_=Wh_words.bitcast(I32).rearrange("g p n -> p g n")
+        )
+        for quadrant in range(4):
+            rows = slice(4 * quadrant, 4 * quadrant + 4)
+            live = slice(32 * quadrant, 32 * quadrant + 4)
+            nc.sync.dma_start(out=w_planes[live, 0, :].bitcast(I32), in_=Wi_scales.bitcast(I32)[0, rows, :])
+            nc.sync.dma_start(
+                out=w_planes[live, 1:PASSES, :].bitcast(I32),
+                in_=Wh_scales.bitcast(I32)[:, rows, :].rearrange("g r n -> r g n"),
+            )
+
+        a_codes = keep.tile([P, M_TILES, PASSES, P], U32, align_bytes=64)
+        a_scales = keep.tile([P, M_TILES, PASSES, P], U8, align_bytes=64)
+        x_words = x_sb[:].bitcast(F32)
+        h_words = h_sb[:].bitcast(F32)
+
+        def word_transpose(dst, words, u):
+            nc.tensor.transpose(dst, words[:, u:PASS_WORDS:2], ident_f32[:])
+
+        def regroup(t_ps):
+            grouped = stage.tile([P, 2, P, 2], F32, align_bytes=64)
+            nc.scalar.copy(out=grouped[:], in_=t_ps[:].rearrange("p o u b -> p o b u"))
+            return grouped
+
+        def quantise(values, codes, scales):
+            nc.vector.quantize_mx(out=codes.bitcast(FP8X4), scales=scales, in_=values.bitcast(BF16))
+
+        for pair in range(M_TILES // 2):
+            x_t = psum_t.tile([P, 2, 2, P], F32, tag="t")
+            for o in range(2):
+                for u in range(2):
+                    word_transpose(x_t[:, o, u, :], x_words[:, 2 * pair + o, :], u)
+            grouped = regroup(x_t)
+            for o in range(2):
+                m = 2 * pair + o
+                quantise(
+                    grouped[:, o, :, :].rearrange("p b u -> p (b u)"), a_codes[:, m, 0, :], a_scales[:, m, 0, :]
+                )
+
+        bias_sum = keep.tile([P, HDIM], F32)
+        for n in range(N_TILES):
+            cols = slice(n * N_TILE, (n + 1) * N_TILE)
+            b_ps = psum_acc.tile([P, N_TILE], F32, tag="acc")
+            nc.tensor.matmul(b_ps[:], lhsT=ones[:], rhs=bias_rows[:, cols], start=True, stop=True)
+            nc.vector.tensor_copy(out=bias_sum[:, cols], in_=b_ps[:])
+
+        st_T = keep.tile([P, M_TILES, NTOP, P], BF16)
+        for pair in range(M_TILES // 2):
+            st_t = psum_t.tile([P, 2, NTOP, P], BF16, tag="t")
+            for o in range(2):
+                for t in range(NTOP):
+                    nc.tensor.transpose(st_t[:, o, t, :], st_sb[:, 2 * pair + o, t, :], ident_bf16[:])
+            nc.vector.tensor_copy(out=st_T[:, 2 * pair : 2 * pair + 2, :, :], in_=st_t[:])
+        w_T = keep.tile([P, NTOP, HDIM], BF16)
+        blocks = N_TILE // P
+        for t in range(NTOP):
+            for n in range(N_TILES):
+                w_t = psum_t.tile([P, blocks, P], BF16, tag="t")
+                for j in range(blocks):
+                    nc.tensor.transpose(w_t[:, j, :], w_sb[:, t, n * blocks + j, :], ident_bf16[:])
+                nc.vector.tensor_copy(
+                    out=w_T[:, t, n * N_TILE : (n + 1) * N_TILE], in_=w_t[:].rearrange("s j h -> s (j h)")
+                )
+
+        pre = keep.tile([P, M_TILES, HDIM], F32)
+        h_grouped = {}
+
+        def quantise_hidden(m):
+            quantise(
+                h_grouped[m][:].rearrange("p g b u -> p (g b u)"),
+                a_codes[:, m, 1:PASSES, :].rearrange("p g b -> p (g b)"),
+                a_scales[:, m, 1:PASSES, :].rearrange("p g b -> p (g b)"),
+            )
+
+        for m in range(M_TILES):
+            h_t = psum_t.tile([P, H_PASSES, 2, P], F32, tag="t")
+            for n in range(N_TILES):
+                cols = slice(n * N_TILE, (n + 1) * N_TILE)
+                acc = psum_acc.tile([P, N_TILE], F32, tag="acc")
+                for t in range(NTOP):
+                    nc.tensor.matmul(
+                        acc[:], lhsT=st_T[:, m, t, :], rhs=w_T[:, t, cols], start=(t == 0), stop=(t == NTOP - 1)
+                    )
+                    g, u = n, t
+                    word_transpose(h_t[:, g, u, :], h_words[:, m, g * PASS_WORDS : (g + 1) * PASS_WORDS], u)
+                nc.vector.tensor_tensor(out=pre[:, m, cols], in0=acc[:], in1=bias_sum[:, cols], op=add)
+            h_grouped[m] = regroup(h_t)
+            if m > 0:
+                quantise_hidden(m - 1)
+        quantise_hidden(M_TILES - 1)
+
+        out_rows = out.rearrange("(p m) h -> p m h", m=M_TILES)
+        for m in range(M_TILES):
+            for n in range(N_TILES):
+                cols = slice(n * N_TILE, (n + 1) * N_TILE)
+                acc = psum_acc.tile([P, N_TILE], F32, tag="acc")
+                for g in range(PASSES):
+                    nc.tensor.matmul_mx(
+                        out=acc[:],
+                        lhsT=a_codes[:, m, g, :].bitcast(FP8X4),
+                        lhsT_scale=a_scales[:, m, g, :],
+                        rhs=w_words[:, g, 2 * n * N_TILE : 2 * (n + 1) * N_TILE].bitcast(FP4X4),
+                        rhs_scale=w_planes[:, g, cols],
+                        start=(g == 0),
+                        stop=(g == PASSES - 1),
+                    )
+                nc.vector.tensor_tensor(out=pre[:, m, cols], in0=acc[:], in1=pre[:, m, cols], op=add)
+                nc.scalar.activation(out=pre[:, m, cols], in_=pre[:, m, cols], func=sigmoid)
+                nc.sync.dma_start(out=out_rows[:, m, cols], in_=pre[:, m, cols])

@@ -20,9 +20,10 @@ K_PASS = 4 * P
 PASSES = (IDIM + HDIM) // K_PASS
 H_PASSES = HDIM // K_PASS
 PASS_WORDS = K_PASS // 2
-H_BLOCKS = HDIM // P
-
-assert N_TILES == H_PASSES and NTOP == 2
+J = N_TILE // P
+MM_SPLIT = 2
+MM_N = N_TILE // MM_SPLIT
+WARM_UP = 4
 
 FLOPS = 2 * BATCH * HDIM * (IDIM + HDIM + NTOP * S)
 
@@ -37,40 +38,50 @@ def tile_stackrnn_pa_kernel(
     with ExitStack() as ctx:
         ctx.enter_context(tc.manual_schedule())
         keep = ctx.enter_context(tc.tile_pool(name="keep", bufs=1))
-        stage = ctx.enter_context(tc.tile_pool(name="stage", bufs=3))
-        psum_t = ctx.enter_context(tc.psum_pool(name="psum_t", bufs=3))
-        psum_acc = ctx.enter_context(tc.psum_pool(name="psum_acc", bufs=5))
+        psum = ctx.enter_context(tc.psum_pool(name="psum", bufs=8))
 
-        ident_f32 = keep.tile([P, P], F32)
-        make_identity(nc, ident_f32[:])
-        ident_bf16 = keep.tile([P, P], BF16)
-        make_identity(nc, ident_bf16[:])
         bias_rows = keep.tile([P, HDIM], BF16)
         nc.vector.memset(bias_rows[:], 0.0)
-        warm = keep.tile([P, 1], F32)
-        nc.vector.memset(warm[:], 0.0)
         ones = keep.tile([P, P], BF16)
         nc.vector.memset(ones[:], 1.0)
+        zeros = keep.tile([P, N_TILE], BF16)
+        nc.vector.memset(zeros[:], 0.0)
+        warm = keep.tile([P, 1], F32)
+        nc.vector.memset(warm[:], 0.0)
         w_planes = keep.tile([P, PASSES, HDIM], U8, align_bytes=64)
         nc.vector.memset(w_planes[:].bitcast(I32), 0)
+        ident_bf16 = keep.tile([P, P], BF16)
+        make_identity(nc, ident_bf16[:])
+        ident_f32 = keep.tile([P, P], F32)
+        make_identity(nc, ident_f32[:])
 
         for row, bias in enumerate((bi, bh, b0, b1)):
             nc.scalar.dma_start(out=bias_rows[row : row + 1, :], in_=bias.rearrange("(o n) -> o n", o=1))
         nc.scalar.activation(out=warm[:], in_=warm[:], func=sigmoid)
+
+        w_sb = keep.tile([P, NTOP, N_TILES, J, S], BF16)
+        w_rows = [w.rearrange("(n p j) s -> n p j s", n=N_TILES, j=J) for w in (W0, W1)]
+        st_sb = keep.tile([P, M_TILES, NTOP, S], BF16)
+        st_rows = stack_top.rearrange("(p m) t s -> p m t s", m=M_TILES)
+
+        def load_w(n):
+            for t in range(NTOP):
+                nc.sync.dma_start(out=w_sb[:, t, n, :, :], in_=w_rows[t][n])
+
+        def load_st(m0, m1):
+            nc.sync.dma_start(out=st_sb[:, m0:m1, :, :], in_=st_rows[:, m0:m1, :, :])
+
+        load_w(0)
+        load_st(0, 2)
+        load_st(2, 4)
+        load_w(1)
+        load_st(4, 8)
 
         x_sb = keep.tile([P, M_TILES, IDIM], BF16)
         x_rows = x.rearrange("(p m) k -> p m k", m=M_TILES)
         for pair in range(M_TILES // 2):
             two = slice(2 * pair, 2 * pair + 2)
             nc.sync.dma_start(out=x_sb[:, two, :], in_=x_rows[:, two, :])
-
-        st_sb = keep.tile([P, M_TILES, NTOP, S], BF16)
-        nc.sync.dma_start(out=st_sb[:], in_=stack_top.rearrange("(p m) t s -> p m t s", m=M_TILES))
-
-        w_sb = keep.tile([P, NTOP, H_BLOCKS, S], BF16)
-        nc.sync.dma_start(out=w_sb[:, 0, :, :], in_=W0.rearrange("(j p) s -> p j s", p=P))
-        nc.sync.dma_start(out=w_sb[:, 1, :, :], in_=W1.rearrange("(j p) s -> p j s", p=P))
-
         h_sb = keep.tile([P, M_TILES, HDIM], BF16)
         h_rows = hidden.rearrange("(p m) k -> p m k", m=M_TILES)
         for pair in range(M_TILES // 2):
@@ -91,101 +102,186 @@ def tile_stackrnn_pa_kernel(
                 in_=Wh_scales.bitcast(I32)[:, rows, :].rearrange("g r n -> r g n"),
             )
 
-        a_codes = keep.tile([P, M_TILES, PASSES, P], U32, align_bytes=64)
-        a_scales = keep.tile([P, M_TILES, PASSES, P], U8, align_bytes=64)
+        st_T = keep.tile([P, M_TILES, NTOP, P], BF16)
+        w_T = keep.tile([P, NTOP, N_TILES, J, P], BF16)
+        bias_sum = keep.tile([P, HDIM], F32)
+        pre = keep.tile([P, M_TILES, HDIM], F32)
+        WORD_BANKS = M_TILES // 2 + M_TILES
+        grouped = keep.tile([P, WORD_BANKS, 2, P, 2], F32, align_bytes=64)
+        x_codes = keep.tile([P, M_TILES, P], U32, align_bytes=64)
+        x_scales = keep.tile([P, M_TILES, P], U8, align_bytes=64)
+        h_codes = keep.tile([P, M_TILES, H_PASSES, P], U32, align_bytes=64)
+        h_scales = keep.tile([P, M_TILES, H_PASSES, P], U8, align_bytes=64)
         x_words = x_sb[:].bitcast(F32)
         h_words = h_sb[:].bitcast(F32)
 
-        def word_transpose(dst, words, u):
-            nc.tensor.transpose(dst, words[:, u:PASS_WORDS:2], ident_f32[:])
+        pending = []
+        clock = {"step": 0}
 
-        def regroup(t_ps):
-            grouped = stage.tile([P, 2, P, 2], F32, align_bytes=64)
-            nc.scalar.copy(out=grouped[:], in_=t_ps[:].rearrange("p o u b -> p o b u"))
-            return grouped
-
-        def quantise(values, codes, scales):
-            nc.vector.quantize_mx(out=codes.bitcast(FP8X4), scales=scales, in_=values.bitcast(BF16))
-
-        for pair in range(M_TILES // 2):
-            x_t = psum_t.tile([P, 2, 2, P], F32, tag="t")
-            for o in range(2):
-                for u in range(2):
-                    word_transpose(x_t[:, o, u, :], x_words[:, 2 * pair + o, :], u)
-            grouped = regroup(x_t)
-            for o in range(2):
-                m = 2 * pair + o
-                quantise(
-                    grouped[:, o, :, :].rearrange("p b u -> p (b u)"), a_codes[:, m, 0, :], a_scales[:, m, 0, :]
-                )
-
-        bias_sum = keep.tile([P, HDIM], F32)
-        for n in range(N_TILES):
-            cols = slice(n * N_TILE, (n + 1) * N_TILE)
-            b_ps = psum_acc.tile([P, N_TILE], F32, tag="acc")
-            nc.tensor.matmul(b_ps[:], lhsT=ones[:], rhs=bias_rows[:, cols], start=True, stop=True)
-            nc.vector.tensor_copy(out=bias_sum[:, cols], in_=b_ps[:])
-
-        st_T = keep.tile([P, M_TILES, NTOP, P], BF16)
-        for pair in range(M_TILES // 2):
-            st_t = psum_t.tile([P, 2, NTOP, P], BF16, tag="t")
-            for o in range(2):
-                for t in range(NTOP):
-                    nc.tensor.transpose(st_t[:, o, t, :], st_sb[:, 2 * pair + o, t, :], ident_bf16[:])
-            nc.vector.tensor_copy(out=st_T[:, 2 * pair : 2 * pair + 2, :, :], in_=st_t[:])
-        w_T = keep.tile([P, NTOP, HDIM], BF16)
-        blocks = N_TILE // P
-        for t in range(NTOP):
-            for n in range(N_TILES):
-                w_t = psum_t.tile([P, blocks, P], BF16, tag="t")
-                for j in range(blocks):
-                    nc.tensor.transpose(w_t[:, j, :], w_sb[:, t, n * blocks + j, :], ident_bf16[:])
-                nc.vector.tensor_copy(
-                    out=w_T[:, t, n * N_TILE : (n + 1) * N_TILE], in_=w_t[:].rearrange("s j h -> s (j h)")
-                )
-
-        pre = keep.tile([P, M_TILES, HDIM], F32)
-        h_grouped = {}
-
-        def quantise_hidden(m):
-            quantise(
-                h_grouped[m][:].rearrange("p g b u -> p (g b u)"),
-                a_codes[:, m, 1:PASSES, :].rearrange("p g b -> p (g b)"),
-                a_scales[:, m, 1:PASSES, :].rearrange("p g b -> p (g b)"),
+        def quantise(k, codes, scales):
+            nc.vector.quantize_mx(
+                out=codes.bitcast(FP8X4),
+                scales=scales,
+                in_=grouped[:, k, :, :, :].rearrange("p o b u -> p (o b u)").bitcast(BF16),
             )
 
-        for m in range(M_TILES):
-            h_t = psum_t.tile([P, H_PASSES, 2, P], F32, tag="t")
-            for n in range(N_TILES):
-                cols = slice(n * N_TILE, (n + 1) * N_TILE)
-                acc = psum_acc.tile([P, N_TILE], F32, tag="acc")
+        def pop_quantise():
+            if pending and pending[0][0] < clock["step"]:
+                pending.pop(0)[1]()
+
+        def w_job(t, n, engine):
+            def empty(bank):
+                engine(out=w_T[:, t, n, :, :], in_=bank[:])
+
+            return (BF16, [w_sb[:, t, n, j, :] for j in range(J)], empty)
+
+        def st_job(pair, engine):
+            def empty(bank):
+                engine(
+                    out=st_T[:, 2 * pair : 2 * pair + 2, :, :].rearrange("s m t b -> s (m t) b"), in_=bank[:]
+                )
+
+            return (BF16, [st_sb[:, 2 * pair + o, t, :] for o in range(2) for t in range(NTOP)], empty)
+
+        def regroup(bank, k):
+            nc.scalar.copy(out=grouped[:, k, :, :, :], in_=bank[:].rearrange("p (o u) b -> p o b u", u=2))
+
+        def x_job(pair):
+            k = pair
+
+            def empty(bank):
+                regroup(bank, k)
+                two = slice(2 * pair, 2 * pair + 2)
+                pending.append(
+                    (
+                        clock["step"],
+                        lambda: quantise(
+                            k,
+                            x_codes[:, two, :].rearrange("p m b -> p (m b)"),
+                            x_scales[:, two, :].rearrange("p m b -> p (m b)"),
+                        ),
+                    )
+                )
+
+            return (F32, [x_words[:, 2 * pair + o, u:PASS_WORDS:2] for o in range(2) for u in range(2)], empty)
+
+        def h_job(m):
+            k = M_TILES // 2 + m
+
+            def empty(bank):
+                regroup(bank, k)
+                pending.append(
+                    (
+                        clock["step"],
+                        lambda: quantise(
+                            k,
+                            h_codes[:, m, :, :].rearrange("p g b -> p (g b)"),
+                            h_scales[:, m, :, :].rearrange("p g b -> p (g b)"),
+                        ),
+                    )
+                )
+
+            return (
+                F32,
+                [h_words[:, m, g * PASS_WORDS + u : (g + 1) * PASS_WORDS : 2] for g in range(H_PASSES) for u in range(2)],
+                empty,
+            )
+
+        open_bank = {}
+
+        def transpose_of(job, i):
+            dtype, sources, empty = job
+            if i == 0:
+                t_bank = psum.tile([P, 4, P], dtype, tag="bank")
+                open_bank["t"] = t_bank
+            t_bank = open_bank["t"]
+            nc.tensor.transpose(t_bank[:, i, :], sources[i], ident_bf16[:] if dtype == BF16 else ident_f32[:])
+            if i == 3:
+                empty(t_bank)
+
+        def whole_job(job):
+            for i in range(4):
+                transpose_of(job, i)
+
+        def bias_matmul(n):
+            cols = slice(n * N_TILE, (n + 1) * N_TILE)
+            b_ps = psum.tile([P, N_TILE], F32, tag="bank")
+            nc.tensor.matmul(b_ps[:], lhsT=ones[:], rhs=bias_rows[:, cols], start=True, stop=True)
+            nc.scalar.copy(out=bias_sum[:, cols], in_=b_ps[:])
+
+        dummy = psum.tile([P, N_TILE], F32, tag="bank")
+        for i in range(WARM_UP):
+            nc.tensor.matmul(dummy[:], lhsT=ones[:], rhs=zeros[:], start=True, stop=True)
+        whole_job(w_job(0, 0, nc.scalar.copy))
+        whole_job(w_job(1, 0, nc.vector.tensor_copy))
+        whole_job(st_job(0, nc.scalar.copy))
+        bias_matmul(0)
+        bias_matmul(1)
+
+        short_jobs = [
+            st_job(1, nc.scalar.copy),
+            w_job(0, 1, nc.scalar.copy),
+            w_job(1, 1, nc.scalar.copy),
+            st_job(2, nc.scalar.copy),
+            st_job(3, nc.scalar.copy),
+        ]
+        word_jobs = [x_job(pair) for pair in range(M_TILES // 2)] + [h_job(m) for m in range(M_TILES)]
+        slots = []
+        for job in short_jobs:
+            slots.append([(job, 0), (job, 1)])
+            slots.append([(job, 2), (job, 3)])
+        for job in word_jobs:
+            for i in range(4):
+                slots.append([(job, i)])
+
+        first = [(m, 0) for m in range(4)] + [(m, 1) for m in range(4)]
+        rest = [(m, n) for m in range(4, M_TILES) for n in range(N_TILES)]
+        for step, (m, n) in enumerate(first + rest):
+            clock["step"] = step
+            cols = slice(n * N_TILE, (n + 1) * N_TILE)
+            acc = psum.tile([P, N_TILE], F32, tag="bank")
+            rhs_all = w_T[:, :, n, :, :].rearrange("s t j c -> s t (j c)")
+            for part in range(MM_SPLIT):
+                part_cols = slice(part * MM_N, (part + 1) * MM_N)
                 for t in range(NTOP):
                     nc.tensor.matmul(
-                        acc[:], lhsT=st_T[:, m, t, :], rhs=w_T[:, t, cols], start=(t == 0), stop=(t == NTOP - 1)
+                        acc[:, part_cols],
+                        lhsT=st_T[:, m, t, :],
+                        rhs=rhs_all[:, t, part_cols],
+                        start=(t == 0),
+                        stop=(t == NTOP - 1),
                     )
-                    g, u = n, t
-                    word_transpose(h_t[:, g, u, :], h_words[:, m, g * PASS_WORDS : (g + 1) * PASS_WORDS], u)
-                nc.vector.tensor_tensor(out=pre[:, m, cols], in0=acc[:], in1=bias_sum[:, cols], op=add)
-            h_grouped[m] = regroup(h_t)
-            if m > 0:
-                quantise_hidden(m - 1)
-        quantise_hidden(M_TILES - 1)
+                    if slots:
+                        for job, i in slots.pop(0):
+                            transpose_of(job, i)
+            nc.vector.tensor_tensor(
+                out=pre[:, m, cols].rearrange("b (c j) -> b c j", j=J),
+                in0=acc[:].rearrange("b (j c) -> b c j", j=J),
+                in1=bias_sum[:, cols].rearrange("b (c j) -> b c j", j=J),
+                op=add,
+            )
+            if step % 2 == 1:
+                pop_quantise()
+        assert not slots
 
+        clock["step"] = len(first + rest)
         out_rows = out.rearrange("(p m) h -> p m h", m=M_TILES)
         for m in range(M_TILES):
             for n in range(N_TILES):
                 cols = slice(n * N_TILE, (n + 1) * N_TILE)
-                acc = psum_acc.tile([P, N_TILE], F32, tag="acc")
+                acc = psum.tile([P, N_TILE], F32, tag="bank")
                 for g in range(PASSES):
                     nc.tensor.matmul_mx(
                         out=acc[:],
-                        lhsT=a_codes[:, m, g, :].bitcast(FP8X4),
-                        lhsT_scale=a_scales[:, m, g, :],
+                        lhsT=(x_codes[:, m, :] if g == 0 else h_codes[:, m, g - 1, :]).bitcast(FP8X4),
+                        lhsT_scale=(x_scales[:, m, :] if g == 0 else h_scales[:, m, g - 1, :]),
                         rhs=w_words[:, g, 2 * n * N_TILE : 2 * (n + 1) * N_TILE].bitcast(FP4X4),
                         rhs_scale=w_planes[:, g, cols],
                         start=(g == 0),
                         stop=(g == PASSES - 1),
                     )
                 nc.vector.tensor_tensor(out=pre[:, m, cols], in0=acc[:], in1=pre[:, m, cols], op=add)
+                pop_quantise()
                 nc.scalar.activation(out=pre[:, m, cols], in_=pre[:, m, cols], func=sigmoid)
                 nc.sync.dma_start(out=out_rows[:, m, cols], in_=pre[:, m, cols])
+        assert not pending

@@ -21,7 +21,7 @@ PASSES = (IDIM + HDIM) // K_PASS
 H_PASSES = HDIM // K_PASS
 PASS_WORDS = K_PASS // 2
 J = N_TILE // P
-MM_SPLIT = 2
+MM_SPLIT = 1
 MM_N = N_TILE // MM_SPLIT
 WARM_UP = 4
 
@@ -226,13 +226,7 @@ def tile_stackrnn_pa_kernel(
             st_job(3, nc.scalar.copy),
         ]
         word_jobs = [x_job(pair) for pair in range(M_TILES // 2)] + [h_job(m) for m in range(M_TILES)]
-        slots = []
-        for job in short_jobs:
-            slots.append([(job, 0), (job, 1)])
-            slots.append([(job, 2), (job, 3)])
-        for job in word_jobs:
-            for i in range(4):
-                slots.append([(job, i)])
+        runs = [short_jobs[0:3], short_jobs[3:5]] + [word_jobs[i : i + 2] for i in range(0, len(word_jobs), 2)]
 
         first = [(m, 0) for m in range(4)] + [(m, 1) for m in range(4)]
         rest = [(m, n) for m in range(4, M_TILES) for n in range(N_TILES)]
@@ -251,18 +245,17 @@ def tile_stackrnn_pa_kernel(
                         start=(t == 0),
                         stop=(t == NTOP - 1),
                     )
-                    if slots:
-                        for job, i in slots.pop(0):
-                            transpose_of(job, i)
             nc.vector.tensor_tensor(
                 out=pre[:, m, cols].rearrange("b (c j) -> b c j", j=J),
                 in0=acc[:].rearrange("b (j c) -> b c j", j=J),
                 in1=bias_sum[:, cols].rearrange("b (c j) -> b c j", j=J),
                 op=add,
             )
+            pop_quantise()
             if step % 2 == 1:
-                pop_quantise()
-        assert not slots
+                for job in runs.pop(0):
+                    whole_job(job)
+        assert not runs
 
         clock["step"] = len(first + rest)
         out_rows = out.rearrange("(p m) h -> p m h", m=M_TILES)

@@ -23,7 +23,7 @@ PASS_WORDS = K_PASS // 2
 J = N_TILE // P
 MM_SPLIT = 1
 MM_N = N_TILE // MM_SPLIT
-WARM_UP = 4
+WARM_UP = 12
 
 FLOPS = 2 * BATCH * HDIM * (IDIM + HDIM + NTOP * S)
 
@@ -40,12 +40,10 @@ def tile_stackrnn_pa_kernel(
         keep = ctx.enter_context(tc.tile_pool(name="keep", bufs=1))
         psum = ctx.enter_context(tc.psum_pool(name="psum", bufs=8))
 
-        bias_rows = keep.tile([P, HDIM], BF16)
-        nc.vector.memset(bias_rows[:], 0.0)
         ones = keep.tile([P, P], BF16)
         nc.vector.memset(ones[:], 1.0)
-        zeros = keep.tile([P, N_TILE], BF16)
-        nc.vector.memset(zeros[:], 0.0)
+        bias_rows = keep.tile([P, HDIM], BF16)
+        nc.vector.memset(bias_rows[:].bitcast(I32), 0)
         warm = keep.tile([P, 1], F32)
         nc.vector.memset(warm[:], 0.0)
         w_planes = keep.tile([P, PASSES, HDIM], U8, align_bytes=64)
@@ -211,7 +209,7 @@ def tile_stackrnn_pa_kernel(
 
         dummy = psum.tile([P, N_TILE], F32, tag="bank")
         for i in range(WARM_UP):
-            nc.tensor.matmul(dummy[:], lhsT=ones[:], rhs=zeros[:], start=True, stop=True)
+            nc.tensor.matmul(dummy[:, 0:P], lhsT=ones[:], rhs=ones[:], start=True, stop=True)
         whole_job(w_job(0, 0, nc.scalar.copy))
         whole_job(w_job(1, 0, nc.vector.tensor_copy))
         whole_job(st_job(0, nc.scalar.copy))
@@ -259,22 +257,23 @@ def tile_stackrnn_pa_kernel(
 
         clock["step"] = len(first + rest)
         out_rows = out.rearrange("(p m) h -> p m h", m=M_TILES)
-        for m in range(M_TILES):
-            for n in range(N_TILES):
-                cols = slice(n * N_TILE, (n + 1) * N_TILE)
-                acc = psum.tile([P, N_TILE], F32, tag="bank")
-                for g in range(PASSES):
-                    nc.tensor.matmul_mx(
-                        out=acc[:],
-                        lhsT=(x_codes[:, m, :] if g == 0 else h_codes[:, m, g - 1, :]).bitcast(FP8X4),
-                        lhsT_scale=(x_scales[:, m, :] if g == 0 else h_scales[:, m, g - 1, :]),
-                        rhs=w_words[:, g, 2 * n * N_TILE : 2 * (n + 1) * N_TILE].bitcast(FP4X4),
-                        rhs_scale=w_planes[:, g, cols],
-                        start=(g == 0),
-                        stop=(g == PASSES - 1),
-                    )
-                nc.vector.tensor_tensor(out=pre[:, m, cols], in0=acc[:], in1=pre[:, m, cols], op=add)
-                pop_quantise()
-                nc.scalar.activation(out=pre[:, m, cols], in_=pre[:, m, cols], func=sigmoid)
-                nc.sync.dma_start(out=out_rows[:, m, cols], in_=pre[:, m, cols])
+        groups = [(m, c0, N_TILE) for m in range(M_TILES) for c0 in range(0, HDIM, N_TILE)][:-1]
+        groups += [(M_TILES - 1, c0, P) for c0 in range(HDIM - N_TILE, HDIM, P)]
+        for m, c0, width in groups:
+            cols = slice(c0, c0 + width)
+            acc = psum.tile([P, width], F32, tag="bank")
+            for g in range(PASSES):
+                nc.tensor.matmul_mx(
+                    out=acc[:],
+                    lhsT=(x_codes[:, m, :] if g == 0 else h_codes[:, m, g - 1, :]).bitcast(FP8X4),
+                    lhsT_scale=(x_scales[:, m, :] if g == 0 else h_scales[:, m, g - 1, :]),
+                    rhs=w_words[:, g, 2 * c0 : 2 * (c0 + width)].bitcast(FP4X4),
+                    rhs_scale=w_planes[:, g, cols],
+                    start=(g == 0),
+                    stop=(g == PASSES - 1),
+                )
+            nc.vector.tensor_tensor(out=pre[:, m, cols], in0=acc[:], in1=pre[:, m, cols], op=add)
+            pop_quantise()
+            nc.scalar.activation(out=pre[:, m, cols], in_=pre[:, m, cols], func=sigmoid)
+            nc.sync.dma_start(out=out_rows[:, m, cols], in_=pre[:, m, cols])
         assert not pending

@@ -112,6 +112,20 @@ def tile_stackrnn_pa_kernel(
         h_scales = keep.tile([P, M_TILES, H_PASSES, P], U8, align_bytes=64)
         x_words = x_sb[:].bitcast(F32)
         h_words = h_sb[:].bitcast(F32)
+        H_SORTED = 4
+        x_sorted = keep.tile([P, M_TILES, 2, P], F32)
+        h_sorted = keep.tile([P, H_SORTED, H_PASSES, 2, P], F32)
+
+        def sort_x(pair):
+            two = slice(2 * pair, 2 * pair + 2)
+            nc.vector.tensor_copy(
+                out=x_sorted[:, two, :, :], in_=x_words[:, two, :].rearrange("p m (w u) -> p m u w", u=2)
+            )
+
+        def sort_h(m):
+            nc.scalar.copy(
+                out=h_sorted[:, m, :, :, :], in_=h_words[:, m, :].rearrange("p (g w u) -> p g u w", g=H_PASSES, u=2)
+            )
 
         pending = []
         clock = {"step": 0}
@@ -161,7 +175,7 @@ def tile_stackrnn_pa_kernel(
                     )
                 )
 
-            return (F32, [x_words[:, 2 * pair + o, u:PASS_WORDS:2] for o in range(2) for u in range(2)], empty)
+            return (F32, [x_sorted[:, 2 * pair + o, u, :] for o in range(2) for u in range(2)], empty)
 
         def h_job(m):
             k = M_TILES // 2 + m
@@ -179,11 +193,15 @@ def tile_stackrnn_pa_kernel(
                     )
                 )
 
-            return (
-                F32,
-                [h_words[:, m, g * PASS_WORDS + u : (g + 1) * PASS_WORDS : 2] for g in range(H_PASSES) for u in range(2)],
-                empty,
-            )
+            if m < H_SORTED:
+                sources = [h_sorted[:, m, g, u, :] for g in range(H_PASSES) for u in range(2)]
+            else:
+                sources = [
+                    h_words[:, m, g * PASS_WORDS + u : (g + 1) * PASS_WORDS : 2]
+                    for g in range(H_PASSES)
+                    for u in range(2)
+                ]
+            return (F32, sources, empty)
 
         open_bank = {}
 
@@ -250,9 +268,14 @@ def tile_stackrnn_pa_kernel(
                 op=add,
             )
             pop_quantise()
+            if 1 <= step <= M_TILES // 2:
+                sort_x(step - 1)
             if step % 2 == 1:
                 for job in runs.pop(0):
                     whole_job(job)
+                if step in (3, 5):
+                    sort_h(step - 3)
+                    sort_h(step - 2)
         assert not runs
 
         clock["step"] = len(first + rest)

@@ -21,8 +21,6 @@ PASSES = (IDIM + HDIM) // K_PASS
 H_PASSES = HDIM // K_PASS
 PASS_WORDS = K_PASS // 2
 J = N_TILE // P
-MM_SPLIT = 1
-MM_N = N_TILE // MM_SPLIT
 WARM_UP = 12
 
 FLOPS = 2 * BATCH * HDIM * (IDIM + HDIM + NTOP * S)
@@ -42,38 +40,34 @@ def tile_stackrnn_pa_kernel(
 
         ones = keep.tile([P, P], BF16)
         nc.vector.memset(ones[:], 1.0)
+        warm = keep.tile([P, 1], F32)
+        nc.scalar.activation(out=warm[:], in_=ones[:, 0:1], func=sigmoid)
         bias_rows = keep.tile([P, HDIM], BF16)
         nc.vector.memset(bias_rows[:].bitcast(I32), 0)
-        warm = keep.tile([P, 1], F32)
-        nc.vector.memset(warm[:], 0.0)
         w_planes = keep.tile([P, PASSES, HDIM], U8, align_bytes=64)
         nc.vector.memset(w_planes[:].bitcast(I32), 0)
-        ident_bf16 = keep.tile([P, P], BF16)
-        make_identity(nc, ident_bf16[:])
         ident_f32 = keep.tile([P, P], F32)
         make_identity(nc, ident_f32[:])
 
-        for row, bias in enumerate((bi, bh, b0, b1)):
-            nc.scalar.dma_start(out=bias_rows[row : row + 1, :], in_=bias.rearrange("(o n) -> o n", o=1))
-        nc.scalar.activation(out=warm[:], in_=warm[:], func=sigmoid)
 
-        w_sb = keep.tile([P, NTOP, N_TILES, J, S], BF16)
+        w_sb = keep.tile([P, N_TILES, J, NTOP, S], BF16)
         w_rows = [w.rearrange("(n p j) s -> n p j s", n=N_TILES, j=J) for w in (W0, W1)]
         st_sb = keep.tile([P, M_TILES, NTOP, S], BF16)
         st_rows = stack_top.rearrange("(p m) t s -> p m t s", m=M_TILES)
 
         def load_w(n):
             for t in range(NTOP):
-                nc.sync.dma_start(out=w_sb[:, t, n, :, :], in_=w_rows[t][n])
+                nc.sync.dma_start(out=w_sb[:, n, :, t, :], in_=w_rows[t][n])
 
         def load_st(m0, m1):
             nc.sync.dma_start(out=st_sb[:, m0:m1, :, :], in_=st_rows[:, m0:m1, :, :])
 
         load_w(0)
         load_st(0, 2)
-        load_st(2, 4)
         load_w(1)
-        load_st(4, 8)
+        load_st(2, 8)
+        for row, bias in enumerate((bi, bh, b0, b1)):
+            nc.sync.dma_start(out=bias_rows[row : row + 1, :], in_=bias.rearrange("(o n) -> o n", o=1))
 
         x_sb = keep.tile([P, M_TILES, IDIM], BF16)
         x_rows = x.rearrange("(p m) k -> p m k", m=M_TILES)
@@ -100,8 +94,12 @@ def tile_stackrnn_pa_kernel(
                 in_=Wh_scales.bitcast(I32)[:, rows, :].rearrange("g r n -> r g n"),
             )
 
-        st_T = keep.tile([P, M_TILES, NTOP, P], BF16)
-        w_T = keep.tile([P, NTOP, N_TILES, J, P], BF16)
+        st_T = keep.tile([P, M_TILES, P], F32)
+        w_T = keep.tile([P, N_TILES, J, P], F32)
+        st_pairs = st_sb[:].bitcast(F32)
+        w_pairs = w_sb[:].bitcast(F32)
+        st_T_halves = st_T[:].bitcast(BF16).rearrange("p m (b e) -> p m e b", e=2)
+        w_T_halves = w_T[:].bitcast(BF16).rearrange("p n j (c e) -> p n e (j c)", e=2)
         bias_sum = keep.tile([P, HDIM], F32)
         pre = keep.tile([P, M_TILES, HDIM], F32)
         WORD_BANKS = M_TILES // 2 + M_TILES
@@ -110,16 +108,20 @@ def tile_stackrnn_pa_kernel(
         x_scales = keep.tile([P, M_TILES, P], U8, align_bytes=64)
         h_codes = keep.tile([P, M_TILES, H_PASSES, P], U32, align_bytes=64)
         h_scales = keep.tile([P, M_TILES, H_PASSES, P], U8, align_bytes=64)
-        x_words = x_sb[:].bitcast(F32)
         h_words = h_sb[:].bitcast(F32)
         H_SORTED = 4
-        x_sorted = keep.tile([P, M_TILES, 2, P], F32)
+        x_sorted = keep.tile([P, M_TILES // 2, 2, 2 * P], F32)
         h_sorted = keep.tile([P, H_SORTED, H_PASSES, 2, P], F32)
 
         def sort_x(pair):
             two = slice(2 * pair, 2 * pair + 2)
-            nc.vector.tensor_copy(
-                out=x_sorted[:, two, :, :], in_=x_words[:, two, :].rearrange("p m (w u) -> p m u w", u=2)
+            nc.gpsimd.tensor_scalar(
+                out=x_sorted[:, pair, :, :].bitcast(BF16).rearrange("p u (w e) -> p u w e", e=2),
+                in0=x_sb[:, two, :].rearrange("p m k -> p (m k)").rearrange("p (w u e) -> p u w e", u=2, e=2),
+                scalar1=1.0,
+                scalar2=0.0,
+                op0=mybir.AluOpType.mult,
+                op1=add,
             )
 
         def sort_h(m):
@@ -141,19 +143,17 @@ def tile_stackrnn_pa_kernel(
             if pending and pending[0][0] < clock["step"]:
                 pending.pop(0)[1]()
 
-        def w_job(t, n, engine):
+        def w_job(n, j0, j1, engine):
             def empty(bank):
-                engine(out=w_T[:, t, n, :, :], in_=bank[:])
+                engine(out=w_T[:, n, j0:j1, :], in_=bank[:])
 
-            return (BF16, [w_sb[:, t, n, j, :] for j in range(J)], empty)
+            return ([w_pairs[:, n, j, :, :].rearrange("p t i -> p (t i)") for j in range(j0, j1)], empty)
 
-        def st_job(pair, engine):
+        def st_job(m0, m1, engine):
             def empty(bank):
-                engine(
-                    out=st_T[:, 2 * pair : 2 * pair + 2, :, :].rearrange("s m t b -> s (m t) b"), in_=bank[:]
-                )
+                engine(out=st_T[:, m0:m1, :], in_=bank[:])
 
-            return (BF16, [st_sb[:, 2 * pair + o, t, :] for o in range(2) for t in range(NTOP)], empty)
+            return ([st_pairs[:, m, :, :].rearrange("p t i -> p (t i)") for m in range(m0, m1)], empty)
 
         def regroup(bank, k):
             nc.scalar.copy(out=grouped[:, k, :, :, :], in_=bank[:].rearrange("p (o u) b -> p o b u", u=2))
@@ -175,7 +175,7 @@ def tile_stackrnn_pa_kernel(
                     )
                 )
 
-            return (F32, [x_sorted[:, 2 * pair + o, u, :] for o in range(2) for u in range(2)], empty)
+            return ([x_sorted[:, pair, u, o * P : (o + 1) * P] for o in range(2) for u in range(2)], empty)
 
         def h_job(m):
             k = M_TILES // 2 + m
@@ -201,66 +201,56 @@ def tile_stackrnn_pa_kernel(
                     for g in range(H_PASSES)
                     for u in range(2)
                 ]
-            return (F32, sources, empty)
-
-        open_bank = {}
-
-        def transpose_of(job, i):
-            dtype, sources, empty = job
-            if i == 0:
-                t_bank = psum.tile([P, 4, P], dtype, tag="bank")
-                open_bank["t"] = t_bank
-            t_bank = open_bank["t"]
-            nc.tensor.transpose(t_bank[:, i, :], sources[i], ident_bf16[:] if dtype == BF16 else ident_f32[:])
-            if i == 3:
-                empty(t_bank)
+            return (sources, empty)
 
         def whole_job(job):
-            for i in range(4):
-                transpose_of(job, i)
+            sources, empty = job
+            t_bank = psum.tile([P, len(sources), P], F32, tag="bank")
+            for i, source in enumerate(sources):
+                nc.tensor.transpose(t_bank[:, i, :], source, ident_f32[:])
+            empty(t_bank)
 
-        def bias_matmul(n):
+        def bias_matmul(n, engine):
             cols = slice(n * N_TILE, (n + 1) * N_TILE)
             b_ps = psum.tile([P, N_TILE], F32, tag="bank")
             nc.tensor.matmul(b_ps[:], lhsT=ones[:], rhs=bias_rows[:, cols], start=True, stop=True)
-            nc.scalar.copy(out=bias_sum[:, cols], in_=b_ps[:])
+            engine(out=bias_sum[:, cols], in_=b_ps[:])
 
         dummy = psum.tile([P, N_TILE], F32, tag="bank")
         for i in range(WARM_UP):
             nc.tensor.matmul(dummy[:, 0:P], lhsT=ones[:], rhs=ones[:], start=True, stop=True)
-        whole_job(w_job(0, 0, nc.scalar.copy))
-        whole_job(w_job(1, 0, nc.vector.tensor_copy))
-        whole_job(st_job(0, nc.scalar.copy))
-        bias_matmul(0)
-        bias_matmul(1)
+        whole_job(w_job(0, 0, 2, nc.scalar.copy))
+        whole_job(w_job(0, 2, 4, nc.vector.tensor_copy))
+        whole_job(st_job(0, 2, nc.scalar.copy))
+        whole_job(w_job(1, 0, 4, nc.vector.tensor_copy))
 
+        for pair in range(M_TILES // 2):
+            sort_x(pair)
+
+        plain_tiles = [(m, n) for m in range(M_TILES) for n in range(N_TILES)]
         short_jobs = [
-            st_job(1, nc.scalar.copy),
-            w_job(0, 1, nc.scalar.copy),
-            w_job(1, 1, nc.scalar.copy),
-            st_job(2, nc.scalar.copy),
-            st_job(3, nc.scalar.copy),
+            st_job(2, 4, nc.scalar.copy),
+            st_job(4, 8, nc.scalar.copy),
         ]
         word_jobs = [x_job(pair) for pair in range(M_TILES // 2)] + [h_job(m) for m in range(M_TILES)]
-        runs = [short_jobs[0:3], short_jobs[3:5]] + [word_jobs[i : i + 2] for i in range(0, len(word_jobs), 2)]
+        runs = {1: short_jobs[0:1], 2: short_jobs[1:2]}
+        for i, job in enumerate(word_jobs):
+            runs[len(plain_tiles) - len(word_jobs) + i] = [job]
 
-        first = [(m, 0) for m in range(4)] + [(m, 1) for m in range(4)]
-        rest = [(m, n) for m in range(4, M_TILES) for n in range(N_TILES)]
-        for step, (m, n) in enumerate(first + rest):
+        for step, (m, n) in enumerate(plain_tiles):
             clock["step"] = step
             cols = slice(n * N_TILE, (n + 1) * N_TILE)
             acc = psum.tile([P, N_TILE], F32, tag="bank")
-            rhs_all = w_T[:, :, n, :, :].rearrange("s t j c -> s t (j c)")
-            for part in range(MM_SPLIT):
-                part_cols = slice(part * MM_N, (part + 1) * MM_N)
-                for t in range(NTOP):
-                    nc.tensor.matmul(
-                        acc[:, part_cols],
-                        lhsT=st_T[:, m, t, :],
-                        rhs=rhs_all[:, t, part_cols],
-                        start=(t == 0),
-                        stop=(t == NTOP - 1),
-                    )
+            for e in range(2):
+                nc.tensor.matmul(
+                    acc[:],
+                    lhsT=st_T_halves[:, m, e, :],
+                    rhs=w_T_halves[:, n, e, :],
+                    start=(e == 0),
+                    stop=(e == 1),
+                )
+            if step < N_TILES:
+                bias_matmul(step, (nc.vector.tensor_copy, nc.scalar.copy)[step])
             nc.vector.tensor_tensor(
                 out=pre[:, m, cols].rearrange("b (c j) -> b c j", j=J),
                 in0=acc[:].rearrange("b (j c) -> b c j", j=J),
@@ -268,17 +258,13 @@ def tile_stackrnn_pa_kernel(
                 op=add,
             )
             pop_quantise()
-            if 1 <= step <= M_TILES // 2:
-                sort_x(step - 1)
-            if step % 2 == 1:
-                for job in runs.pop(0):
-                    whole_job(job)
-                if step in (3, 5):
-                    sort_h(step - 3)
-                    sort_h(step - 2)
-        assert not runs
+            for job in runs.get(step, []):
+                whole_job(job)
+            if step in (4, 6):
+                sort_h(step - 4)
+                sort_h(step - 3)
 
-        clock["step"] = len(first + rest)
+        clock["step"] = len(plain_tiles)
         out_rows = out.rearrange("(p m) h -> p m h", m=M_TILES)
         groups = [(m, c0, N_TILE) for m in range(M_TILES) for c0 in range(0, HDIM, N_TILE)][:-1]
         groups += [(M_TILES - 1, c0, P) for c0 in range(HDIM - N_TILE, HDIM, P)]

@@ -51,7 +51,7 @@ def tile_stackrnn_pa_kernel(
 
 
         w_sb = keep.tile([P, N_TILES, J, NTOP, S], BF16)
-        w_rows = [w.rearrange("(n p j) s -> n p j s", n=N_TILES, j=J) for w in (W0, W1)]
+        w_rows = [w.rearrange("(n j p) s -> n p j s", n=N_TILES, j=J) for w in (W0, W1)]
         st_sb = keep.tile([P, M_TILES, NTOP, S], BF16)
         st_rows = stack_top.rearrange("(p m) t s -> p m t s", m=M_TILES)
 
@@ -251,12 +251,7 @@ def tile_stackrnn_pa_kernel(
                 )
             if step < N_TILES:
                 bias_matmul(step, (nc.vector.tensor_copy, nc.scalar.copy)[step])
-            nc.vector.tensor_tensor(
-                out=pre[:, m, cols].rearrange("b (c j) -> b c j", j=J),
-                in0=acc[:].rearrange("b (j c) -> b c j", j=J),
-                in1=bias_sum[:, cols].rearrange("b (c j) -> b c j", j=J),
-                op=add,
-            )
+            nc.vector.tensor_tensor(out=pre[:, m, cols], in0=acc[:], in1=bias_sum[:, cols], op=add)
             pop_quantise()
             for job in runs.get(step, []):
                 whole_job(job)

@@ -21,7 +21,9 @@ PASSES = (IDIM + HDIM) // K_PASS
 H_PASSES = HDIM // K_PASS
 PASS_WORDS = K_PASS // 2
 J = N_TILE // P
-WARM_UP = 12
+WARM_N = 256
+WARM_UP = 9
+WARM_GAP = 4
 
 FLOPS = 2 * BATCH * HDIM * (IDIM + HDIM + NTOP * S)
 
@@ -38,7 +40,7 @@ def tile_stackrnn_pa_kernel(
         keep = ctx.enter_context(tc.tile_pool(name="keep", bufs=1))
         psum = ctx.enter_context(tc.psum_pool(name="psum", bufs=8))
 
-        ones = keep.tile([P, P], BF16)
+        ones = keep.tile([P, WARM_N], BF16)
         nc.vector.memset(ones[:], 1.0)
         warm = keep.tile([P, 1], F32)
         nc.scalar.activation(out=warm[:], in_=ones[:, 0:1], func=sigmoid)
@@ -213,15 +215,19 @@ def tile_stackrnn_pa_kernel(
         def bias_matmul(n, engine):
             cols = slice(n * N_TILE, (n + 1) * N_TILE)
             b_ps = psum.tile([P, N_TILE], F32, tag="bank")
-            nc.tensor.matmul(b_ps[:], lhsT=ones[:], rhs=bias_rows[:, cols], start=True, stop=True)
+            nc.tensor.matmul(b_ps[:], lhsT=ones[:, 0:P], rhs=bias_rows[:, cols], start=True, stop=True)
             engine(out=bias_sum[:, cols], in_=b_ps[:])
 
-        dummy = psum.tile([P, N_TILE], F32, tag="bank")
-        for i in range(WARM_UP):
-            nc.tensor.matmul(dummy[:, 0:P], lhsT=ones[:], rhs=ones[:], start=True, stop=True)
+        def keep_warm(count):
+            dummy = psum.tile([P, WARM_N], F32, tag="bank")
+            for i in range(count):
+                nc.tensor.matmul(dummy[:], lhsT=ones[:, 0:P], rhs=ones[:], start=True, stop=True)
+
+        keep_warm(WARM_UP)
         whole_job(w_job(0, 0, 2, nc.scalar.copy))
         whole_job(w_job(0, 2, 4, nc.vector.tensor_copy))
         whole_job(st_job(0, 2, nc.scalar.copy))
+        keep_warm(WARM_GAP)
         whole_job(w_job(1, 0, 4, nc.vector.tensor_copy))
 
         for pair in range(M_TILES // 2):

@@ -19,11 +19,10 @@ N_TILES = HDIM // N_TILE
 K_PASS = 4 * P
 PASSES = (IDIM + HDIM) // K_PASS
 H_PASSES = HDIM // K_PASS
-PASS_WORDS = K_PASS // 2
 J = N_TILE // P
 WARM_N = 256
 WARM_UP = 9
-WARM_GAP = 4
+WARM_GAP = 1
 
 FLOPS = 2 * BATCH * HDIM * (IDIM + HDIM + NTOP * S)
 
@@ -66,10 +65,10 @@ def tile_stackrnn_pa_kernel(
 
         load_w(0)
         load_st(0, 2)
-        load_w(1)
-        load_st(2, 8)
         for row, bias in enumerate((bi, bh, b0, b1)):
             nc.sync.dma_start(out=bias_rows[row : row + 1, :], in_=bias.rearrange("(o n) -> o n", o=1))
+        load_w(1)
+        load_st(2, 8)
 
         x_sb = keep.tile([P, M_TILES, IDIM], BF16)
         x_rows = x.rearrange("(p m) k -> p m k", m=M_TILES)
@@ -111,20 +110,33 @@ def tile_stackrnn_pa_kernel(
         h_codes = keep.tile([P, M_TILES, H_PASSES, P], U32, align_bytes=64)
         h_scales = keep.tile([P, M_TILES, H_PASSES, P], U8, align_bytes=64)
         h_words = h_sb[:].bitcast(F32)
-        H_SORTED = 4
+        X_ON_GPSIMD = (2, 3)
+        H_ON_GPSIMD = (4, 5, 6)
         x_sorted = keep.tile([P, M_TILES // 2, 2, 2 * P], F32)
-        h_sorted = keep.tile([P, H_SORTED, H_PASSES, 2, P], F32)
+        h_sorted = keep.tile([P, M_TILES, H_PASSES, 2, P], F32)
+
+        def move_pairs(dst, src):
+            nc.gpsimd.tensor_scalar(
+                out=dst, in0=src, scalar1=1.0, scalar2=0.0, op0=mybir.AluOpType.mult, op1=add
+            )
 
         def sort_x(pair):
             two = slice(2 * pair, 2 * pair + 2)
-            nc.gpsimd.tensor_scalar(
-                out=x_sorted[:, pair, :, :].bitcast(BF16).rearrange("p u (w e) -> p u w e", e=2),
-                in0=x_sb[:, two, :].rearrange("p m k -> p (m k)").rearrange("p (w u e) -> p u w e", u=2, e=2),
-                scalar1=1.0,
-                scalar2=0.0,
-                op0=mybir.AluOpType.mult,
-                op1=add,
+            move_pairs(
+                x_sorted[:, pair, :, :].bitcast(BF16).rearrange("p u (w e) -> p u w e", e=2),
+                x_sb[:, two, :].rearrange("p m k -> p (m k)").rearrange("p (w u e) -> p u w e", u=2, e=2),
             )
+
+        def sort_x_words(pair, engine):
+            words = x_sb[:, 2 * pair : 2 * pair + 2, :].bitcast(F32).rearrange("p m w -> p (m w)")
+            engine(out=x_sorted[:, pair, :, :], in_=words.rearrange("p (w u) -> p u w", u=2))
+
+        def sort_h_on_gpsimd(m):
+            for g in range(H_PASSES):
+                move_pairs(
+                    h_sorted[:, m, g, :, :].bitcast(BF16).rearrange("p u (w e) -> p u w e", e=2),
+                    h_sb[:, m, g * K_PASS : (g + 1) * K_PASS].rearrange("p (w u e) -> p u w e", u=2, e=2),
+                )
 
         def sort_h(m):
             nc.scalar.copy(
@@ -195,15 +207,7 @@ def tile_stackrnn_pa_kernel(
                     )
                 )
 
-            if m < H_SORTED:
-                sources = [h_sorted[:, m, g, u, :] for g in range(H_PASSES) for u in range(2)]
-            else:
-                sources = [
-                    h_words[:, m, g * PASS_WORDS + u : (g + 1) * PASS_WORDS : 2]
-                    for g in range(H_PASSES)
-                    for u in range(2)
-                ]
-            return (sources, empty)
+            return ([h_sorted[:, m, g, u, :] for g in range(H_PASSES) for u in range(2)], empty)
 
         def whole_job(job):
             sources, empty = job
@@ -227,19 +231,25 @@ def tile_stackrnn_pa_kernel(
         whole_job(w_job(0, 0, 2, nc.scalar.copy))
         whole_job(w_job(0, 2, 4, nc.vector.tensor_copy))
         whole_job(st_job(0, 2, nc.scalar.copy))
+        bias_matmul(0, nc.vector.tensor_copy)
+        bias_matmul(1, nc.scalar.copy)
         keep_warm(WARM_GAP)
-        whole_job(w_job(1, 0, 4, nc.vector.tensor_copy))
 
-        for pair in range(M_TILES // 2):
+        for pair in X_ON_GPSIMD:
             sort_x(pair)
+        for m in H_ON_GPSIMD:
+            sort_h_on_gpsimd(m)
 
-        plain_tiles = [(m, n) for m in range(M_TILES) for n in range(N_TILES)]
+        plain_tiles = [(0, 0), (1, 0), (0, 1), (1, 1)]
+        plain_tiles += [(m, n) for m in range(2, M_TILES) for n in range(N_TILES)]
         short_jobs = [
+            w_job(1, 0, 2, nc.vector.tensor_copy),
+            w_job(1, 2, 4, nc.scalar.copy),
             st_job(2, 4, nc.scalar.copy),
             st_job(4, 8, nc.scalar.copy),
         ]
         word_jobs = [x_job(pair) for pair in range(M_TILES // 2)] + [h_job(m) for m in range(M_TILES)]
-        runs = {1: short_jobs[0:1], 2: short_jobs[1:2]}
+        runs = {0: short_jobs[0:2], 1: short_jobs[2:3], 2: short_jobs[3:4]}
         for i, job in enumerate(word_jobs):
             runs[len(plain_tiles) - len(word_jobs) + i] = [job]
 
@@ -255,15 +265,21 @@ def tile_stackrnn_pa_kernel(
                     start=(e == 0),
                     stop=(e == 1),
                 )
-            if step < N_TILES:
-                bias_matmul(step, (nc.vector.tensor_copy, nc.scalar.copy)[step])
+            for job in runs.get(step, []) if step == 0 else []:
+                whole_job(job)
             nc.vector.tensor_tensor(out=pre[:, m, cols], in0=acc[:], in1=bias_sum[:, cols], op=add)
             pop_quantise()
-            for job in runs.get(step, []):
+            for job in runs.get(step, []) if step else []:
                 whole_job(job)
+            if step == 1:
+                sort_x_words(0, nc.scalar.copy)
+            if step == 2:
+                sort_x_words(1, nc.vector.tensor_copy)
             if step in (4, 6):
                 sort_h(step - 4)
                 sort_h(step - 3)
+            if step == 10:
+                sort_h(7)
 
         clock["step"] = len(plain_tiles)
         out_rows = out.rearrange("(p m) h -> p m h", m=M_TILES)
@@ -271,6 +287,7 @@ def tile_stackrnn_pa_kernel(
         groups += [(M_TILES - 1, c0, P) for c0 in range(HDIM - N_TILE, HDIM, P)]
         for m, c0, width in groups:
             cols = slice(c0, c0 + width)
+            step = N_TILE // 2 if (m, c0) == (M_TILES - 1, 0) else width
             acc = psum.tile([P, width], F32, tag="bank")
             for g in range(PASSES):
                 nc.tensor.matmul_mx(
@@ -282,8 +299,12 @@ def tile_stackrnn_pa_kernel(
                     start=(g == 0),
                     stop=(g == PASSES - 1),
                 )
-            nc.vector.tensor_tensor(out=pre[:, m, cols], in0=acc[:], in1=pre[:, m, cols], op=add)
-            pop_quantise()
-            nc.scalar.activation(out=pre[:, m, cols], in_=pre[:, m, cols], func=sigmoid)
-            nc.sync.dma_start(out=out_rows[:, m, cols], in_=pre[:, m, cols])
+            for p0 in range(0, width, step):
+                part = slice(c0 + p0, c0 + p0 + step)
+                nc.vector.tensor_tensor(
+                    out=pre[:, m, part], in0=acc[:, p0 : p0 + step], in1=pre[:, m, part], op=add
+                )
+                pop_quantise()
+                nc.scalar.activation(out=pre[:, m, part], in_=pre[:, m, part], func=sigmoid)
+                nc.sync.dma_start(out=out_rows[:, m, part], in_=pre[:, m, part])
         assert not pending

@@ -17,6 +17,7 @@ M_TILES = BATCH // P
 N_TILE = 512
 N_TILES = HDIM // N_TILE
 K_PASS = 4 * P
+PASS_WORDS = K_PASS // 2
 PASSES = (IDIM + HDIM) // K_PASS
 H_PASSES = HDIM // K_PASS
 J = N_TILE // P
@@ -89,10 +90,10 @@ def tile_stackrnn_pa_kernel(
         for quadrant in range(4):
             rows = slice(4 * quadrant, 4 * quadrant + 4)
             live = slice(32 * quadrant, 32 * quadrant + 4)
-            nc.sync.dma_start(out=w_planes[live, 0, :].bitcast(I32), in_=Wi_scales.bitcast(I32)[0, rows, :])
-            nc.sync.dma_start(
-                out=w_planes[live, 1:PASSES, :].bitcast(I32),
-                in_=Wh_scales.bitcast(I32)[:, rows, :].rearrange("g r n -> r g n"),
+            nc.gpsimd.dma_start(out=w_planes[live, 0, :].bitcast(F32), in_=Wi_scales.bitcast(F32)[0, rows, :])
+            nc.gpsimd.dma_start(
+                out=w_planes[live, 1:PASSES, :].bitcast(F32),
+                in_=Wh_scales.bitcast(F32)[:, rows, :].rearrange("g r n -> r g n"),
             )
 
         st_T = keep.tile([P, M_TILES, P], F32)
@@ -110,21 +111,14 @@ def tile_stackrnn_pa_kernel(
         h_codes = keep.tile([P, M_TILES, H_PASSES, P], U32, align_bytes=64)
         h_scales = keep.tile([P, M_TILES, H_PASSES, P], U8, align_bytes=64)
         h_words = h_sb[:].bitcast(F32)
-        X_ON_GPSIMD = (2, 3)
-        H_ON_GPSIMD = (4, 5, 6)
+        H_ON_GPSIMD = (4,)
+        H_UNSORTED = (5, 6)
         x_sorted = keep.tile([P, M_TILES // 2, 2, 2 * P], F32)
         h_sorted = keep.tile([P, M_TILES, H_PASSES, 2, P], F32)
 
         def move_pairs(dst, src):
             nc.gpsimd.tensor_scalar(
                 out=dst, in0=src, scalar1=1.0, scalar2=0.0, op0=mybir.AluOpType.mult, op1=add
-            )
-
-        def sort_x(pair):
-            two = slice(2 * pair, 2 * pair + 2)
-            move_pairs(
-                x_sorted[:, pair, :, :].bitcast(BF16).rearrange("p u (w e) -> p u w e", e=2),
-                x_sb[:, two, :].rearrange("p m k -> p (m k)").rearrange("p (w u e) -> p u w e", u=2, e=2),
             )
 
         def sort_x_words(pair, engine):
@@ -207,7 +201,15 @@ def tile_stackrnn_pa_kernel(
                     )
                 )
 
-            return ([h_sorted[:, m, g, u, :] for g in range(H_PASSES) for u in range(2)], empty)
+            if m in H_UNSORTED:
+                sources = [
+                    h_words[:, m, g * PASS_WORDS + u : (g + 1) * PASS_WORDS : 2]
+                    for g in range(H_PASSES)
+                    for u in range(2)
+                ]
+            else:
+                sources = [h_sorted[:, m, g, u, :] for g in range(H_PASSES) for u in range(2)]
+            return (sources, empty)
 
         def whole_job(job):
             sources, empty = job
@@ -235,8 +237,6 @@ def tile_stackrnn_pa_kernel(
         bias_matmul(1, nc.scalar.copy)
         keep_warm(WARM_GAP)
 
-        for pair in X_ON_GPSIMD:
-            sort_x(pair)
         for m in H_ON_GPSIMD:
             sort_h_on_gpsimd(m)
 
@@ -271,10 +271,8 @@ def tile_stackrnn_pa_kernel(
             pop_quantise()
             for job in runs.get(step, []) if step else []:
                 whole_job(job)
-            if step == 1:
-                sort_x_words(0, nc.scalar.copy)
-            if step == 2:
-                sort_x_words(1, nc.vector.tensor_copy)
+            if 1 <= step <= 4:
+                sort_x_words(step - 1, nc.scalar.copy if step % 2 else nc.vector.tensor_copy)
             if step in (4, 6):
                 sort_h(step - 4)
                 sort_h(step - 3)

@@ -22,7 +22,7 @@ PASSES = (IDIM + HDIM) // K_PASS
 H_PASSES = HDIM // K_PASS
 J = N_TILE // P
 WARM_N = 256
-WARM_UP = 9
+WARM_UP = 8
 WARM_GAP = 1
 
 FLOPS = 2 * BATCH * HDIM * (IDIM + HDIM + NTOP * S)
@@ -52,14 +52,18 @@ def tile_stackrnn_pa_kernel(
         make_identity(nc, ident_f32[:])
 
 
+        w_raw = keep.tile([P, NTOP, N_TILES, J, S], BF16)
         w_sb = keep.tile([P, N_TILES, J, NTOP, S], BF16)
-        w_rows = [w.rearrange("(n j p) s -> n p j s", n=N_TILES, j=J) for w in (W0, W1)]
+        w_rows = [w.rearrange("(n a p o) s -> n p a o s", n=N_TILES, a=2, o=2) for w in (W0, W1)]
         st_sb = keep.tile([P, M_TILES, NTOP, S], BF16)
         st_rows = stack_top.rearrange("(p m) t s -> p m t s", m=M_TILES)
 
         def load_w(n):
             for t in range(NTOP):
-                nc.sync.dma_start(out=w_sb[:, n, :, t, :], in_=w_rows[t][n])
+                nc.sync.dma_start(
+                    out=w_raw[:, t, n, :, :].rearrange("p (a o) s -> p a (o s)", a=2),
+                    in_=w_rows[t][n].rearrange("p a o s -> p a (o s)"),
+                )
 
         def load_st(m0, m1):
             nc.sync.dma_start(out=st_sb[:, m0:m1, :, :], in_=st_rows[:, m0:m1, :, :])
@@ -97,11 +101,12 @@ def tile_stackrnn_pa_kernel(
             )
 
         st_T = keep.tile([P, M_TILES, P], F32)
-        w_T = keep.tile([P, N_TILES, J, P], F32)
+        w_T = keep.tile([P, N_TILES, N_TILE], F32)
         st_pairs = st_sb[:].bitcast(F32)
         w_pairs = w_sb[:].bitcast(F32)
         st_T_halves = st_T[:].bitcast(BF16).rearrange("p m (b e) -> p m e b", e=2)
-        w_T_halves = w_T[:].bitcast(BF16).rearrange("p n j (c e) -> p n e (j c)", e=2)
+        w_T_halves = w_T[:].bitcast(BF16).rearrange("p n (c e) -> p n e c", e=2)
+        w_raw_pairs = w_raw[:].bitcast(F32)
         bias_sum = keep.tile([P, HDIM], F32)
         pre = keep.tile([P, M_TILES, HDIM], F32)
         WORD_BANKS = M_TILES // 2 + M_TILES
@@ -111,29 +116,16 @@ def tile_stackrnn_pa_kernel(
         h_codes = keep.tile([P, M_TILES, H_PASSES, P], U32, align_bytes=64)
         h_scales = keep.tile([P, M_TILES, H_PASSES, P], U8, align_bytes=64)
         h_words = h_sb[:].bitcast(F32)
-        H_ON_GPSIMD = (4,)
         H_UNSORTED = (5, 6)
         x_sorted = keep.tile([P, M_TILES // 2, 2, 2 * P], F32)
         h_sorted = keep.tile([P, M_TILES, H_PASSES, 2, P], F32)
-
-        def move_pairs(dst, src):
-            nc.gpsimd.tensor_scalar(
-                out=dst, in0=src, scalar1=1.0, scalar2=0.0, op0=mybir.AluOpType.mult, op1=add
-            )
 
         def sort_x_words(pair, engine):
             words = x_sb[:, 2 * pair : 2 * pair + 2, :].bitcast(F32).rearrange("p m w -> p (m w)")
             engine(out=x_sorted[:, pair, :, :], in_=words.rearrange("p (w u) -> p u w", u=2))
 
-        def sort_h_on_gpsimd(m):
-            for g in range(H_PASSES):
-                move_pairs(
-                    h_sorted[:, m, g, :, :].bitcast(BF16).rearrange("p u (w e) -> p u w e", e=2),
-                    h_sb[:, m, g * K_PASS : (g + 1) * K_PASS].rearrange("p (w u e) -> p u w e", u=2, e=2),
-                )
-
-        def sort_h(m):
-            nc.scalar.copy(
+        def sort_h(m, engine):
+            engine(
                 out=h_sorted[:, m, :, :, :], in_=h_words[:, m, :].rearrange("p (g w u) -> p g u w", g=H_PASSES, u=2)
             )
 
@@ -151,11 +143,16 @@ def tile_stackrnn_pa_kernel(
             if pending and pending[0][0] < clock["step"]:
                 pending.pop(0)[1]()
 
-        def w_job(n, j0, j1, engine):
-            def empty(bank):
-                engine(out=w_T[:, n, j0:j1, :], in_=bank[:])
+        def join_w(n):
+            for t, engine in enumerate((nc.vector.tensor_copy, nc.scalar.copy)):
+                engine(out=w_pairs[:, n, :, t, :], in_=w_raw_pairs[:, t, n, :, :])
 
-            return ([w_pairs[:, n, j, :, :].rearrange("p t i -> p (t i)") for j in range(j0, j1)], empty)
+        def w_job(n, a, engine):
+            def empty(bank):
+                half = w_T[:, n, 2 * a * P : 2 * (a + 1) * P]
+                engine(out=half.rearrange("p (c o) -> p c o", o=2), in_=bank[:].rearrange("p o c -> p c o"))
+
+            return ([w_pairs[:, n, 2 * a + o, :, :].rearrange("p t i -> p (t i)") for o in range(2)], empty)
 
         def st_job(m0, m1, engine):
             def empty(bank):
@@ -230,21 +227,20 @@ def tile_stackrnn_pa_kernel(
                 nc.tensor.matmul(dummy[:], lhsT=ones[:, 0:P], rhs=ones[:], start=True, stop=True)
 
         keep_warm(WARM_UP)
-        whole_job(w_job(0, 0, 2, nc.scalar.copy))
-        whole_job(w_job(0, 2, 4, nc.vector.tensor_copy))
+        join_w(0)
         whole_job(st_job(0, 2, nc.scalar.copy))
+        whole_job(w_job(0, 0, nc.vector.tensor_copy))
+        whole_job(w_job(0, 1, nc.scalar.copy))
+        join_w(1)
         bias_matmul(0, nc.vector.tensor_copy)
         bias_matmul(1, nc.scalar.copy)
         keep_warm(WARM_GAP)
 
-        for m in H_ON_GPSIMD:
-            sort_h_on_gpsimd(m)
-
         plain_tiles = [(0, 0), (1, 0), (0, 1), (1, 1)]
         plain_tiles += [(m, n) for m in range(2, M_TILES) for n in range(N_TILES)]
         short_jobs = [
-            w_job(1, 0, 2, nc.vector.tensor_copy),
-            w_job(1, 2, 4, nc.scalar.copy),
+            w_job(1, 0, nc.vector.tensor_copy),
+            w_job(1, 1, nc.scalar.copy),
             st_job(2, 4, nc.scalar.copy),
             st_job(4, 8, nc.scalar.copy),
         ]
@@ -274,10 +270,12 @@ def tile_stackrnn_pa_kernel(
             if 1 <= step <= 4:
                 sort_x_words(step - 1, nc.scalar.copy if step % 2 else nc.vector.tensor_copy)
             if step in (4, 6):
-                sort_h(step - 4)
-                sort_h(step - 3)
+                sort_h(step - 4, nc.scalar.copy)
+                sort_h(step - 3, nc.scalar.copy)
+            if step == 8:
+                sort_h(4, nc.vector.tensor_copy)
             if step == 10:
-                sort_h(7)
+                sort_h(7, nc.scalar.copy)
 
         clock["step"] = len(plain_tiles)
         out_rows = out.rearrange("(p m) h -> p m h", m=M_TILES)

@@ -45,7 +45,7 @@ def tile_stackrnn_pa_kernel(
         warm = keep.tile([P, 1], F32)
         nc.scalar.activation(out=warm[:], in_=ones[:, 0:1], func=sigmoid)
         bias_rows = keep.tile([P, HDIM], BF16)
-        nc.vector.memset(bias_rows[:].bitcast(I32), 0)
+        nc.gpsimd.memset(bias_rows[:].bitcast(F32), 0.0)
         w_planes = keep.tile([P, PASSES, HDIM], U8, align_bytes=64)
         nc.vector.memset(w_planes[:].bitcast(I32), 0)
         ident_f32 = keep.tile([P, P], F32)
@@ -116,9 +116,21 @@ def tile_stackrnn_pa_kernel(
         h_codes = keep.tile([P, M_TILES, H_PASSES, P], U32, align_bytes=64)
         h_scales = keep.tile([P, M_TILES, H_PASSES, P], U8, align_bytes=64)
         h_words = h_sb[:].bitcast(F32)
-        H_UNSORTED = (5, 6)
+        H_ON_GPSIMD = (4, 5)
+        H_UNSORTED = (6,)
         x_sorted = keep.tile([P, M_TILES // 2, 2, 2 * P], F32)
         h_sorted = keep.tile([P, M_TILES, H_PASSES, 2, P], F32)
+
+        def sort_h_on_gpsimd(m):
+            for g in range(H_PASSES):
+                nc.gpsimd.tensor_scalar(
+                    out=h_sorted[:, m, g, :, :].bitcast(BF16).rearrange("p u (w e) -> p u w e", e=2),
+                    in0=h_sb[:, m, g * K_PASS : (g + 1) * K_PASS].rearrange("p (w u e) -> p u w e", u=2, e=2),
+                    scalar1=1.0,
+                    scalar2=0.0,
+                    op0=mybir.AluOpType.mult,
+                    op1=add,
+                )
 
         def sort_x_words(pair, engine):
             words = x_sb[:, 2 * pair : 2 * pair + 2, :].bitcast(F32).rearrange("p m w -> p (m w)")
@@ -238,13 +250,16 @@ def tile_stackrnn_pa_kernel(
 
         plain_tiles = [(0, 0), (1, 0), (0, 1), (1, 1)]
         plain_tiles += [(m, n) for m in range(2, M_TILES) for n in range(N_TILES)]
+        H_ORDER = (0, 1, 2, 3, 6, 4, 7, 5)
+        for m in H_ON_GPSIMD:
+            sort_h_on_gpsimd(m)
         short_jobs = [
             w_job(1, 0, nc.vector.tensor_copy),
             w_job(1, 1, nc.scalar.copy),
             st_job(2, 4, nc.scalar.copy),
             st_job(4, 8, nc.scalar.copy),
         ]
-        word_jobs = [x_job(pair) for pair in range(M_TILES // 2)] + [h_job(m) for m in range(M_TILES)]
+        word_jobs = [x_job(pair) for pair in range(M_TILES // 2)] + [h_job(m) for m in H_ORDER]
         runs = {0: short_jobs[0:2], 1: short_jobs[2:3], 2: short_jobs[3:4]}
         for i, job in enumerate(word_jobs):
             runs[len(plain_tiles) - len(word_jobs) + i] = [job]
@@ -272,8 +287,6 @@ def tile_stackrnn_pa_kernel(
             if step in (4, 6):
                 sort_h(step - 4, nc.scalar.copy)
                 sort_h(step - 3, nc.scalar.copy)
-            if step == 8:
-                sort_h(4, nc.vector.tensor_copy)
             if step == 10:
                 sort_h(7, nc.scalar.copy)
 

from contextlib import ExitStack

import concourse.mybir as mybir
from concourse.masks import make_identity

F32 = mybir.dt.float32
BF16 = mybir.dt.bfloat16
I32 = mybir.dt.int32
U32 = mybir.dt.uint32
U8 = mybir.dt.uint8
FP8X4 = mybir.dt.float8_e4m3fn_x4
FP4X4 = mybir.dt.float4_e2m1fn_x4

P = 128
BATCH, IDIM, HDIM, S, NTOP = 1024, 512, 1024, 128, 2
M_TILES = BATCH // P
N_TILE = 512
N_TILES = HDIM // N_TILE
K_PASS = 4 * P
PASS_WORDS = K_PASS // 2
PASSES = (IDIM + HDIM) // K_PASS
H_PASSES = HDIM // K_PASS
J = N_TILE // P
WARM_N = 256
WARM_UP = 8
WARM_GAP = 1

FLOPS = 2 * BATCH * HDIM * (IDIM + HDIM + NTOP * S)


def tile_stackrnn_pa_kernel(
    tc, x, hidden, stack_top, Wi_words, Wi_scales, bi, Wh_words, Wh_scales, bh, W0, b0, W1, b1, out
):
    nc = tc.nc
    add = mybir.AluOpType.add
    sigmoid = mybir.ActivationFunctionType.Sigmoid

    with ExitStack() as ctx:
        ctx.enter_context(tc.manual_schedule())
        keep = ctx.enter_context(tc.tile_pool(name="keep", bufs=1))
        psum = ctx.enter_context(tc.psum_pool(name="psum", bufs=8))

        ones = keep.tile([P, WARM_N], BF16)
        nc.vector.memset(ones[:], 1.0)
        warm = keep.tile([P, 1], F32)
        nc.scalar.activation(out=warm[:], in_=ones[:, 0:1], func=sigmoid)
        bias_rows = keep.tile([P, HDIM], BF16)
        nc.gpsimd.memset(bias_rows[:].bitcast(F32), 0.0)
        w_planes = keep.tile([P, PASSES, HDIM], U8, align_bytes=64)
        nc.vector.memset(w_planes[:].bitcast(I32), 0)
        ident_f32 = keep.tile([P, P], F32)
        make_identity(nc, ident_f32[:])


        w_raw = keep.tile([P, NTOP, N_TILES, J, S], BF16)
        w_sb = keep.tile([P, N_TILES, J, NTOP, S], BF16)
        w_rows = [w.rearrange("(n a p o) s -> n p a o s", n=N_TILES, a=2, o=2) for w in (W0, W1)]
        st_sb = keep.tile([P, M_TILES, NTOP, S], BF16)
        st_rows = stack_top.rearrange("(p m) t s -> p m t s", m=M_TILES)

        def load_w(n):
            for t in range(NTOP):
                nc.sync.dma_start(
                    out=w_raw[:, t, n, :, :].rearrange("p (a o) s -> p a (o s)", a=2),
                    in_=w_rows[t][n].rearrange("p a o s -> p a (o s)"),
                )

        def load_st(m0, m1):
            nc.sync.dma_start(out=st_sb[:, m0:m1, :, :], in_=st_rows[:, m0:m1, :, :])

        load_w(0)
        load_st(0, 2)
        for row, bias in enumerate((bi, bh, b0, b1)):
            nc.sync.dma_start(out=bias_rows[row : row + 1, :], in_=bias.rearrange("(o n) -> o n", o=1))
        load_w(1)
        load_st(2, 8)

        x_sb = keep.tile([P, M_TILES, IDIM], BF16)
        x_rows = x.rearrange("(p m) k -> p m k", m=M_TILES)
        for pair in range(M_TILES // 2):
            two = slice(2 * pair, 2 * pair + 2)
            nc.sync.dma_start(out=x_sb[:, two, :], in_=x_rows[:, two, :])
        h_sb = keep.tile([P, M_TILES, HDIM], BF16)
        h_rows = hidden.rearrange("(p m) k -> p m k", m=M_TILES)
        for pair in range(M_TILES // 2):
            two = slice(2 * pair, 2 * pair + 2)
            nc.sync.dma_start(out=h_sb[:, two, :], in_=h_rows[:, two, :])

        w_words = keep.tile([P, PASSES, 2 * HDIM], U8, align_bytes=64)
        nc.sync.dma_start(out=w_words[:, 0, :].bitcast(I32), in_=Wi_words.bitcast(I32)[0])
        nc.sync.dma_start(
            out=w_words[:, 1:PASSES, :].bitcast(I32), in_=Wh_words.bitcast(I32).rearrange("g p n -> p g n")
        )
        for quadrant in range(4):
            rows = slice(4 * quadrant, 4 * quadrant + 4)
            live = slice(32 * quadrant, 32 * quadrant + 4)
            nc.gpsimd.dma_start(out=w_planes[live, 0, :].bitcast(F32), in_=Wi_scales.bitcast(F32)[0, rows, :])
            nc.gpsimd.dma_start(
                out=w_planes[live, 1:PASSES, :].bitcast(F32),
                in_=Wh_scales.bitcast(F32)[:, rows, :].rearrange("g r n -> r g n"),
            )

        st_T = keep.tile([P, M_TILES, P], F32)
        w_T = keep.tile([P, N_TILES, N_TILE], F32)
        st_pairs = st_sb[:].bitcast(F32)
        w_pairs = w_sb[:].bitcast(F32)
        st_T_halves = st_T[:].bitcast(BF16).rearrange("p m (b e) -> p m e b", e=2)
        w_T_halves = w_T[:].bitcast(BF16).rearrange("p n (c e) -> p n e c", e=2)
        w_raw_pairs = w_raw[:].bitcast(F32)
        bias_sum = keep.tile([P, HDIM], F32)
        pre = keep.tile([P, M_TILES, HDIM], F32)
        WORD_BANKS = M_TILES // 2 + M_TILES
        grouped = keep.tile([P, WORD_BANKS, 2, P, 2], F32, align_bytes=64)
        x_codes = keep.tile([P, M_TILES, P], U32, align_bytes=64)
        x_scales = keep.tile([P, M_TILES, P], U8, align_bytes=64)
        h_codes = keep.tile([P, M_TILES, H_PASSES, P], U32, align_bytes=64)
        h_scales = keep.tile([P, M_TILES, H_PASSES, P], U8, align_bytes=64)
        h_words = h_sb[:].bitcast(F32)
        H_ON_GPSIMD = (4, 5)
        H_UNSORTED = (6,)
        x_sorted = keep.tile([P, M_TILES // 2, 2, 2 * P], F32)
        h_sorted = keep.tile([P, M_TILES, H_PASSES, 2, P], F32)

        def sort_h_on_gpsimd(m):
            for g in range(H_PASSES):
                nc.gpsimd.tensor_scalar(
                    out=h_sorted[:, m, g, :, :].bitcast(BF16).rearrange("p u (w e) -> p u w e", e=2),
                    in0=h_sb[:, m, g * K_PASS : (g + 1) * K_PASS].rearrange("p (w u e) -> p u w e", u=2, e=2),
                    scalar1=1.0,
                    scalar2=0.0,
                    op0=mybir.AluOpType.mult,
                    op1=add,
                )

        def sort_x_words(pair, engine):
            words = x_sb[:, 2 * pair : 2 * pair + 2, :].bitcast(F32).rearrange("p m w -> p (m w)")
            engine(out=x_sorted[:, pair, :, :], in_=words.rearrange("p (w u) -> p u w", u=2))

        def sort_h(m, engine):
            engine(
                out=h_sorted[:, m, :, :, :], in_=h_words[:, m, :].rearrange("p (g w u) -> p g u w", g=H_PASSES, u=2)
            )

        pending = []
        clock = {"step": 0}

        def quantise(k, codes, scales):
            nc.vector.quantize_mx(
                out=codes.bitcast(FP8X4),
                scales=scales,
                in_=grouped[:, k, :, :, :].rearrange("p o b u -> p (o b u)").bitcast(BF16),
            )

        def pop_quantise():
            if pending and pending[0][0] < clock["step"]:
                pending.pop(0)[1]()

        def join_w(n):
            for t, engine in enumerate((nc.vector.tensor_copy, nc.scalar.copy)):
                engine(out=w_pairs[:, n, :, t, :], in_=w_raw_pairs[:, t, n, :, :])

        def w_job(n, a, engine):
            def empty(bank):
                half = w_T[:, n, 2 * a * P : 2 * (a + 1) * P]
                engine(out=half.rearrange("p (c o) -> p c o", o=2), in_=bank[:].rearrange("p o c -> p c o"))

            return ([w_pairs[:, n, 2 * a + o, :, :].rearrange("p t i -> p (t i)") for o in range(2)], empty)

        def st_job(m0, m1, engine):
            def empty(bank):
                engine(out=st_T[:, m0:m1, :], in_=bank[:])

            return ([st_pairs[:, m, :, :].rearrange("p t i -> p (t i)") for m in range(m0, m1)], empty)

        def regroup(bank, k):
            nc.scalar.copy(out=grouped[:, k, :, :, :], in_=bank[:].rearrange("p (o u) b -> p o b u", u=2))

        def x_job(pair):
            k = pair

            def empty(bank):
                regroup(bank, k)
                two = slice(2 * pair, 2 * pair + 2)
                pending.append(
                    (
                        clock["step"],
                        lambda: quantise(
                            k,
                            x_codes[:, two, :].rearrange("p m b -> p (m b)"),
                            x_scales[:, two, :].rearrange("p m b -> p (m b)"),
                        ),
                    )
                )

            return ([x_sorted[:, pair, u, o * P : (o + 1) * P] for o in range(2) for u in range(2)], empty)

        def h_job(m):
            k = M_TILES // 2 + m

            def empty(bank):
                regroup(bank, k)
                pending.append(
                    (
                        clock["step"],
                        lambda: quantise(
                            k,
                            h_codes[:, m, :, :].rearrange("p g b -> p (g b)"),
                            h_scales[:, m, :, :].rearrange("p g b -> p (g b)"),
                        ),
                    )
                )

            if m in H_UNSORTED:
                sources = [
                    h_words[:, m, g * PASS_WORDS + u : (g + 1) * PASS_WORDS : 2]
                    for g in range(H_PASSES)
                    for u in range(2)
                ]
            else:
                sources = [h_sorted[:, m, g, u, :] for g in range(H_PASSES) for u in range(2)]
            return (sources, empty)

        def whole_job(job):
            sources, empty = job
            t_bank = psum.tile([P, len(sources), P], F32, tag="bank")
            for i, source in enumerate(sources):
                nc.tensor.transpose(t_bank[:, i, :], source, ident_f32[:])
            empty(t_bank)

        def bias_matmul(n, engine):
            cols = slice(n * N_TILE, (n + 1) * N_TILE)
            b_ps = psum.tile([P, N_TILE], F32, tag="bank")
            nc.tensor.matmul(b_ps[:], lhsT=ones[:, 0:P], rhs=bias_rows[:, cols], start=True, stop=True)
            engine(out=bias_sum[:, cols], in_=b_ps[:])

        def keep_warm(count):
            dummy = psum.tile([P, WARM_N], F32, tag="bank")
            for i in range(count):
                nc.tensor.matmul(dummy[:], lhsT=ones[:, 0:P], rhs=ones[:], start=True, stop=True)

        keep_warm(WARM_UP)
        join_w(0)
        whole_job(st_job(0, 2, nc.scalar.copy))
        whole_job(w_job(0, 0, nc.vector.tensor_copy))
        whole_job(w_job(0, 1, nc.scalar.copy))
        join_w(1)
        bias_matmul(0, nc.vector.tensor_copy)
        bias_matmul(1, nc.scalar.copy)
        keep_warm(WARM_GAP)

        plain_tiles = [(0, 0), (1, 0), (0, 1), (1, 1)]
        plain_tiles += [(m, n) for m in range(2, M_TILES) for n in range(N_TILES)]
        H_ORDER = (0, 1, 2, 3, 6, 4, 7, 5)
        for m in H_ON_GPSIMD:
            sort_h_on_gpsimd(m)
        short_jobs = [
            w_job(1, 0, nc.vector.tensor_copy),
            w_job(1, 1, nc.scalar.copy),
            st_job(2, 4, nc.scalar.copy),
            st_job(4, 8, nc.scalar.copy),
        ]
        word_jobs = [x_job(pair) for pair in range(M_TILES // 2)] + [h_job(m) for m in H_ORDER]
        runs = {0: short_jobs[0:2], 1: short_jobs[2:3], 2: short_jobs[3:4]}
        for i, job in enumerate(word_jobs):
            runs[len(plain_tiles) - len(word_jobs) + i] = [job]

        for step, (m, n) in enumerate(plain_tiles):
            clock["step"] = step
            cols = slice(n * N_TILE, (n + 1) * N_TILE)
            acc = psum.tile([P, N_TILE], F32, tag="bank")
            for e in range(2):
                nc.tensor.matmul(
                    acc[:],
                    lhsT=st_T_halves[:, m, e, :],
                    rhs=w_T_halves[:, n, e, :],
                    start=(e == 0),
                    stop=(e == 1),
                )
            for job in runs.get(step, []) if step == 0 else []:
                whole_job(job)
            nc.vector.tensor_tensor(out=pre[:, m, cols], in0=acc[:], in1=bias_sum[:, cols], op=add)
            pop_quantise()
            for job in runs.get(step, []) if step else []:
                whole_job(job)
            if 1 <= step <= 4:
                sort_x_words(step - 1, nc.scalar.copy if step % 2 else nc.vector.tensor_copy)
            if step in (4, 6):
                sort_h(step - 4, nc.scalar.copy)
                sort_h(step - 3, nc.scalar.copy)
            if step == 10:
                sort_h(7, nc.scalar.copy)

        clock["step"] = len(plain_tiles)
        out_rows = out.rearrange("(p m) h -> p m h", m=M_TILES)
        groups = [(m, c0, N_TILE) for m in range(M_TILES) for c0 in range(0, HDIM, N_TILE)][:-1]
        groups += [(M_TILES - 1, c0, P) for c0 in range(HDIM - N_TILE, HDIM, P)]
        for m, c0, width in groups:
            cols = slice(c0, c0 + width)
            step = N_TILE // 2 if (m, c0) == (M_TILES - 1, 0) else width
            acc = psum.tile([P, width], F32, tag="bank")
            for g in range(PASSES):
                nc.tensor.matmul_mx(
                    out=acc[:],
                    lhsT=(x_codes[:, m, :] if g == 0 else h_codes[:, m, g - 1, :]).bitcast(FP8X4),
                    lhsT_scale=(x_scales[:, m, :] if g == 0 else h_scales[:, m, g - 1, :]),
                    rhs=w_words[:, g, 2 * c0 : 2 * (c0 + width)].bitcast(FP4X4),
                    rhs_scale=w_planes[:, g, cols],
                    start=(g == 0),
                    stop=(g == PASSES - 1),
                )
            for p0 in range(0, width, step):
                part = slice(c0 + p0, c0 + p0 + step)
                nc.vector.tensor_tensor(
                    out=pre[:, m, part], in0=acc[:, p0 : p0 + step], in1=pre[:, m, part], op=add
                )
                pop_quantise()
                nc.scalar.activation(out=pre[:, m, part], in_=pre[:, m, part], func=sigmoid)
                nc.sync.dma_start(out=out_rows[:, m, part], in_=pre[:, m, part])
        assert not pending
